import numpy as np
import ml_dtypes


def mxq(x, axis, fmt="e4m3"):
    dtype, down = {"e4m3": (ml_dtypes.float8_e4m3fn, 7), "e5m2": (ml_dtypes.float8_e5m2, 14)}[fmt]
    v = np.moveaxis(np.asarray(x, np.float32).astype(ml_dtypes.bfloat16).astype(np.float64), axis, -1)
    blocks = v.reshape(v.shape[:-1] + (-1, 32))
    amax = np.abs(blocks).max(-1, keepdims=True)
    byte = np.maximum(np.where(amax > 0, np.frexp(amax)[1] - 1 + 127, 0) - down, 1)
    scale = np.exp2(byte - 127.0)
    codes = (blocks / scale).astype(np.float32).astype(dtype).astype(np.float64)
    return np.moveaxis((codes * scale).reshape(v.shape), -1, axis)


WIDE = False


def mx_kscale(k):
    if not WIDE:
        return np.ones(k)
    levels = np.array([10, -10, 5, -5, 0])
    if k % 512:
        return np.exp2(np.random.permutation(np.resize(levels, k // 32))).repeat(32)
    a = np.empty((k // 512, 16))
    for p in range(k // 512):
        a[p, :8] = np.random.permutation(np.resize(levels, 8))
        for g in range(8):
            far = levels[np.abs(levels - a[p, g]) >= 10]
            a[p, g + 8] = far[np.random.randint(len(far))]
    return np.exp2(a.ravel()).repeat(32)


BF16 = ml_dtypes.bfloat16


def bf(x):
    return np.asarray(x, np.float32).astype(BF16)


def f64(x):
    return np.asarray(x).astype(np.float64)


B, N, IN_DIM, OUT_DIM, K = 4, 1024, 1024, 128, 3
EPS = 1e-6
SIG = 2.0


def laplacian(adj):
    d = adj.sum(axis=2)
    r = (d + EPS) ** -0.5
    return np.eye(N)[None] - r[:, :, None] * adj * r[:, None, :]


def setup_inputs():
    s = mx_kscale(N)
    return {"x": bf(np.random.standard_normal((B, N, IN_DIM)) * (s / s.max())[:, None]),
            "adj": bf(np.exp(SIG * np.random.standard_normal((B, N, N)) - SIG * SIG / 2.0) / N * (s * s)[:, None])}


def reference(x, adj):
    L = laplacian(f64(adj))
    return mxq(L, 2, "e4m3") @ mxq(f64(x), 1, "e4m3")

@@ -1,0 +1,277 @@
+from contextlib import ExitStack
+
+import concourse.mybir as mybir
+from concourse.masks import make_identity
+
+F32 = mybir.dt.float32
+BF16 = mybir.dt.bfloat16
+U32 = mybir.dt.uint32
+U8 = mybir.dt.uint8
+FP8X4 = mybir.dt.float8_e4m3fn_x4
+ALU = mybir.AluOpType
+ACT = mybir.ActivationFunctionType
+
+GRAPHS = 4
+NODES = 1024
+FEATURES = 1024
+EPS = 1e-6
+
+P = 128
+PACK = 4
+K_PASS = P * PACK
+PASSES = NODES // K_PASS
+PAIR = 2
+HALVES = PACK // PAIR
+ROW_BLOCKS = NODES // P
+GROUP = 2
+ROW_GROUPS = ROW_BLOCKS // GROUP
+STEPS = GRAPHS * ROW_GROUPS
+BANK = 512
+FEATURE_TILES = FEATURES // BANK
+X_WIDTH = PASSES * FEATURES // ROW_GROUPS
+
+LANE = 8
+IN_FLIGHT = 6
+SUM_LEAD = ROW_GROUPS + 4 // GROUP
+X_LEAD = ROW_GROUPS - 1
+
+FLOPS = 2 * GRAPHS * NODES * NODES * FEATURES
+
+
+def scalar_sums(g):
+    return ROW_BLOCKS // 2 if g == 0 else ROW_BLOCKS - 2
+
+
+def sum_column(g, b):
+    return b if b < scalar_sums(g) else LANE + b - scalar_sums(g)
+
+
+def tile_cheblayer_pa_t_kernel(tc, x, adj, out):
+    nc = tc.nc
+    with ExitStack() as ctx:
+        const = ctx.enter_context(tc.tile_pool(name="const", bufs=1))
+        adj_pool = ctx.enter_context(tc.tile_pool(name="adj", bufs=GRAPHS))
+        x_pool = ctx.enter_context(tc.tile_pool(name="x", bufs=GRAPHS))
+        sum_pool = ctx.enter_context(tc.tile_pool(name="sums", bufs=GRAPHS))
+        small = ctx.enter_context(tc.tile_pool(name="small", bufs=2))
+        unread = ctx.enter_context(tc.tile_pool(name="unread", bufs=2))
+        row_pool = ctx.enter_context(tc.tile_pool(name="r_row", bufs=2))
+        diag_pool = ctx.enter_context(tc.tile_pool(name="diag", bufs=4))
+        x_stage = ctx.enter_context(tc.tile_pool(name="x_stage", bufs=2))
+        x_mx = ctx.enter_context(tc.tile_pool(name="x_mx", bufs=2))
+        lap_stage = ctx.enter_context(tc.tile_pool(name="lap_stage", bufs=IN_FLIGHT // GROUP))
+        lap_mx = ctx.enter_context(tc.tile_pool(name="lap_mx", bufs=IN_FLIGHT // GROUP))
+        out_pool = ctx.enter_context(tc.tile_pool(name="out", bufs=IN_FLIGHT))
+        turn_psum = ctx.enter_context(tc.psum_pool(name="turn", bufs=4))
+        acc_psum = ctx.enter_context(tc.psum_pool(name="acc", bufs=4))
+
+        ident = const.tile([P, P], F32)
+        make_identity(nc, ident[:])
+        eps = const.tile([P, 1], F32)
+        nc.vector.memset(eps[:], EPS)
+
+        warm = const.tile([P, 1], F32)
+        nc.scalar.activation(out=warm[:], in_=eps[:], func=ACT.Abs_reciprocal_sqrt)
+
+        adj_of, x_of, sums_of = [], [], []
+        for g in range(GRAPHS):
+            adj_sb = adj_pool.tile([P, ROW_BLOCKS, NODES], BF16)
+            for u in range(ROW_GROUPS):
+                nc.sync.dma_start(
+                    out=adj_sb[:, u * GROUP : (u + 1) * GROUP, :],
+                    in_=adj[g, u * GROUP * P : (u + 1) * GROUP * P, :].rearrange(
+                        "(b p) j -> p b j", p=P
+                    ),
+                )
+            x_sb = x_pool.tile([P, PASSES, PACK, FEATURES], BF16)
+            for s in range(PASSES):
+                nc.sync.dma_start(
+                    out=x_sb[:, s],
+                    in_=x[g, s * K_PASS : (s + 1) * K_PASS, :].rearrange(
+                        "(p t) f -> p t f", t=PACK
+                    ),
+                )
+            sums = sum_pool.tile([P, 2 * LANE], F32)
+            nc.vector.memset(sums[:], 1.0)
+            adj_of.append(adj_sb)
+            x_of.append(x_sb)
+            sums_of.append(sums)
+
+        def sum_rows(g, u):
+            for b in range(u * GROUP, (u + 1) * GROUP):
+                total = sums_of[g][:, sum_column(g, b) : sum_column(g, b) + 1]
+                if b < scalar_sums(g):
+                    scalar_copy = unread.tile([P, NODES], BF16)
+                    nc.scalar.activation(
+                        out=scalar_copy[:], in_=adj_of[g][:, b, :], func=ACT.Copy, accum_out=total
+                    )
+                else:
+                    vector_copy = unread.tile([P, NODES], BF16)
+                    nc.vector.tensor_scalar(
+                        out=vector_copy[:], in0=adj_of[g][:, b, :], scalar1=1.0, scalar2=None,
+                        op0=ALU.mult, op1=ALU.add, accum_out=total,
+                    )
+
+        def guess_scales(g):
+            guess = small.tile([P, 2 * LANE], F32)
+            nc.scalar.activation(
+                out=guess[:], in_=sums_of[g][:], func=ACT.Abs_reciprocal_sqrt, bias=eps[:]
+            )
+            return guess
+
+        def refine_scales(g, guess):
+            half_sq = small.tile([P, 2 * LANE], F32)
+            nc.vector.scalar_tensor_tensor(
+                out=half_sq[:], in0=guess[:], scalar=0.5, in1=guess[:], op0=ALU.mult, op1=ALU.mult
+            )
+            near_half = small.tile([P, 2 * LANE], F32)
+            nc.vector.scalar_tensor_tensor(
+                out=near_half[:], in0=sums_of[g][:], scalar=EPS, in1=half_sq[:],
+                op0=ALU.add, op1=ALU.mult,
+            )
+            neg_r = small.tile([P, 2 * LANE], F32)
+            nc.vector.scalar_tensor_tensor(
+                out=neg_r[:], in0=near_half[:], scalar=1.5, in1=guess[:],
+                op0=ALU.subtract, op1=ALU.mult,
+            )
+            r_row = row_pool.tile([P, NODES], F32)
+            blocks_per_bank = BANK // P
+            for h in range(NODES // BANK):
+                spread = turn_psum.tile([P, blocks_per_bank, P], F32, tag="turn")
+                for q in range(blocks_per_bank):
+                    column = sum_column(g, h * blocks_per_bank + q)
+                    nc.tensor.matmul(
+                        out=spread[:, q, :],
+                        lhsT=neg_r[:, column : column + 1].to_broadcast([P, P]),
+                        rhs=ident[:],
+                        start=True,
+                        stop=True,
+                    )
+                nc.scalar.mul(
+                    out=r_row[:, h * BANK : (h + 1) * BANK],
+                    in_=spread[:].rearrange("p q n -> p (q n)"),
+                    mul=-1.0,
+                )
+            return neg_r, r_row
+
+        def regroup_x(g, q):
+            s, n = divmod(q, ROW_GROUPS // PASSES)
+            grouped = x_stage.tile([P, X_WIDTH, PACK], BF16, align_bytes=64)
+            nc.vector.tensor_copy(
+                out=grouped[:].rearrange("p (c i) t -> p c t i", i=4),
+                in_=x_of[g][:, s, :, n * X_WIDTH : (n + 1) * X_WIDTH].rearrange(
+                    "p t (c i) -> p c t i", i=4
+                ),
+            )
+            return grouped
+
+        def quantise_x(q, grouped, x_codes, x_scales):
+            s, n = divmod(q, ROW_GROUPS // PASSES)
+            cols = slice(n * X_WIDTH, (n + 1) * X_WIDTH)
+            nc.vector.quantize_mx(
+                out=x_codes[:, s, cols].bitcast(FP8X4),
+                scales=x_scales[:, s, cols],
+                in_=grouped[:].rearrange("p f t -> p (f t)"),
+            )
+
+        def form_rows(g, u, neg_r, r_row):
+            adj_sb = adj_of[g]
+            blocks = range(u * GROUP, (u + 1) * GROUP)
+            products = {}
+            for b in blocks:
+                product = diag_pool.tile([P, P], F32)
+                nc.vector.scalar_tensor_tensor(
+                    out=product[:], in0=adj_sb[:, b, b * P : (b + 1) * P],
+                    scalar=neg_r[:, sum_column(g, b) : sum_column(g, b) + 1],
+                    in1=r_row[:, b * P : (b + 1) * P], op0=ALU.mult, op1=ALU.mult,
+                )
+                products[b] = product
+            for b in blocks:
+                for lo, hi in ((0, b * P), ((b + 1) * P, NODES)):
+                    if lo < hi:
+                        nc.vector.scalar_tensor_tensor(
+                            out=adj_sb[:, b, lo:hi], in0=adj_sb[:, b, lo:hi],
+                            scalar=neg_r[:, sum_column(g, b) : sum_column(g, b) + 1],
+                            in1=r_row[:, lo:hi], op0=ALU.mult, op1=ALU.mult,
+                        )
+                nc.vector.tensor_add(
+                    out=adj_sb[:, b, b * P : (b + 1) * P], in0=products[b][:], in1=ident[:]
+                )
+
+        def turn_rows(g, u):
+            words = adj_of[g][:].bitcast(F32).rearrange(
+                "p b (s w h) -> p b s h w", s=PASSES, h=HALVES
+            )
+            grouped = lap_stage.tile([P, GROUP, PASSES, P, HALVES], F32, align_bytes=64)
+            for b in range(GROUP):
+                turned = turn_psum.tile([P, PASSES, HALVES, P], F32, tag="turn")
+                for s in range(PASSES):
+                    for h in range(HALVES):
+                        nc.tensor.transpose(
+                            turned[:, s, h, :], words[:, u * GROUP + b, s, h, :], ident[:]
+                        )
+                nc.scalar.copy(out=grouped[:, b], in_=turned[:].rearrange("p s h m -> p s m h"))
+            return grouped
+
+        def quantise_rows(grouped):
+            lap_codes = lap_mx.tile([P, GROUP * PASSES * P], U32, align_bytes=64)
+            lap_scales = lap_mx.tile([P, GROUP * PASSES * P], U8, align_bytes=64)
+            nc.vector.quantize_mx(
+                out=lap_codes[:].bitcast(FP8X4),
+                scales=lap_scales[:],
+                in_=grouped[:].rearrange("p b s m h -> p (b s m h)").bitcast(BF16),
+            )
+            return lap_codes, lap_scales
+
+        def multiply_and_store(g, u, lap_codes, lap_scales, x_codes, x_scales):
+            for b in range(GROUP):
+                result = out_pool.tile([P, FEATURES], F32)
+                for n in range(FEATURE_TILES):
+                    cols = slice(n * BANK, (n + 1) * BANK)
+                    acc = acc_psum.tile([P, BANK], F32)
+                    for s in range(PASSES):
+                        rows = slice((b * PASSES + s) * P, (b * PASSES + s + 1) * P)
+                        nc.tensor.matmul_mx(
+                            out=acc[:],
+                            lhsT=lap_codes[:, rows].bitcast(FP8X4),
+                            lhsT_scale=lap_scales[:, rows],
+                            rhs=x_codes[:, s, cols].bitcast(FP8X4),
+                            rhs_scale=x_scales[:, s, cols],
+                            start=(s == 0),
+                            stop=(s == PASSES - 1),
+                        )
+                    nc.scalar.copy(out=result[:, cols], in_=acc[:])
+                first_row = (u * GROUP + b) * P
+                nc.sync.dma_start(out=out[g, first_row : first_row + P, :], in_=result[:])
+
+        guess_of, scales_of, x_mx_of = {}, {}, {}
+        grouped_of = {}
+        for step in range(-SUM_LEAD, STEPS + 1):
+            g, u = divmod(step + SUM_LEAD, ROW_GROUPS)
+            if g < GRAPHS:
+                sum_rows(g, u)
+                if u == ROW_GROUPS - 1:
+                    guess_of[g] = guess_scales(g)
+            if u == 0 and 0 < g <= GRAPHS:
+                scales_of[g - 1] = refine_scales(g - 1, guess_of[g - 1])
+
+            x_g, x_q = divmod(step + X_LEAD, ROW_GROUPS)
+            x_due = 0 <= step + X_LEAD < STEPS
+            if x_due:
+                if x_q == 0:
+                    x_codes = x_mx.tile([P, PASSES, FEATURES], U32, align_bytes=64)
+                    x_scales = x_mx.tile([P, PASSES, FEATURES], U8, align_bytes=64)
+                    x_mx_of[x_g] = (x_codes, x_scales)
+                x_grouped = regroup_x(x_g, x_q)
+
+            if 0 <= step < STEPS:
+                g, u = divmod(step, ROW_GROUPS)
+                form_rows(g, u, *scales_of[g])
+                grouped_of[step] = turn_rows(g, u)
+            if 0 <= step - 1:
+                lap_codes, lap_scales = quantise_rows(grouped_of[step - 1])
+            if x_due:
+                quantise_x(x_q, x_grouped, *x_mx_of[x_g])
+            if 0 <= step - 1:
+                g, u = divmod(step - 1, ROW_GROUPS)
+                multiply_and_store(g, u, lap_codes, lap_scales, *x_mx_of[g])

@@ -39,7 +39,7 @@ FLOPS = 2 * GRAPHS * NODES * NODES * FEATURES
 
 
 def scalar_sums(g):
-    return ROW_BLOCKS // 2 if g == 0 else ROW_BLOCKS - 2
+    return ROW_BLOCKS // 2 if g == 0 else ROW_BLOCKS
 
 
 def sum_column(g, b):
@@ -67,6 +67,8 @@ def tile_cheblayer_pa_t_kernel(tc, x, adj, out):
 
         ident = const.tile([P, P], F32)
         make_identity(nc, ident[:])
+        ident_bf16 = const.tile([P, P], BF16)
+        nc.vector.tensor_copy(out=ident_bf16[:], in_=ident[:])
         eps = const.tile([P, 1], F32)
         nc.vector.memset(eps[:], EPS)
 
@@ -112,6 +114,25 @@ def tile_cheblayer_pa_t_kernel(tc, x, adj, out):
                         op0=ALU.mult, op1=ALU.add, accum_out=total,
                     )
 
+        def sum_rows_on_tensor(g, u):
+            folded = turn_psum.tile([P, GROUP, P], F32, tag="turn")
+            for k in range(GROUP):
+                for c in range(ROW_BLOCKS):
+                    nc.tensor.matmul(
+                        out=folded[:, k, :],
+                        lhsT=ident_bf16[:],
+                        rhs=adj_of[g][:, u * GROUP + k, c * P : (c + 1) * P],
+                        start=(c == 0),
+                        stop=(c == ROW_BLOCKS - 1),
+                    )
+            for k in range(GROUP):
+                column = sum_column(g, u * GROUP + k)
+                folded_copy = unread.tile([P, P], F32)
+                nc.scalar.activation(
+                    out=folded_copy[:], in_=folded[:, k, :], func=ACT.Copy,
+                    accum_out=sums_of[g][:, column : column + 1],
+                )
+
         def guess_scales(g):
             guess = small.tile([P, 2 * LANE], F32)
             nc.scalar.activation(
@@ -140,12 +161,10 @@ def tile_cheblayer_pa_t_kernel(tc, x, adj, out):
                 spread = turn_psum.tile([P, blocks_per_bank, P], F32, tag="turn")
                 for q in range(blocks_per_bank):
                     column = sum_column(g, h * blocks_per_bank + q)
-                    nc.tensor.matmul(
-                        out=spread[:, q, :],
-                        lhsT=neg_r[:, column : column + 1].to_broadcast([P, P]),
-                        rhs=ident[:],
-                        start=True,
-                        stop=True,
+                    nc.tensor.transpose(
+                        spread[:, q, :],
+                        neg_r[:, column : column + 1].to_broadcast([P, P]),
+                        ident[:],
                     )
                 nc.scalar.mul(
                     out=r_row[:, h * BANK : (h + 1) * BANK],
@@ -249,7 +268,10 @@ def tile_cheblayer_pa_t_kernel(tc, x, adj, out):
         for step in range(-SUM_LEAD, STEPS + 1):
             g, u = divmod(step + SUM_LEAD, ROW_GROUPS)
             if g < GRAPHS:
-                sum_rows(g, u)
+                if g == 0:
+                    sum_rows(g, u)
+                else:
+                    sum_rows_on_tensor(g, u)
                 if u == ROW_GROUPS - 1:
                     guess_of[g] = guess_scales(g)
             if u == 0 and 0 < g <= GRAPHS:

@@ -32,7 +32,7 @@ X_WIDTH = PASSES * FEATURES // ROW_GROUPS
 
 LANE = 8
 IN_FLIGHT = 6
-SUM_LEAD = ROW_GROUPS + 4 // GROUP
+SUM_LEAD = ROW_GROUPS + 3
 X_LEAD = ROW_GROUPS - 1
 
 FLOPS = 2 * GRAPHS * NODES * NODES * FEATURES
@@ -40,6 +40,16 @@ FLOPS = 2 * GRAPHS * NODES * NODES * FEATURES
 
 def scalar_sums(g):
     return ROW_BLOCKS // 2 if g == 0 else ROW_BLOCKS
+
+
+def scalar_parts(g):
+    return (0, 2) if g == 0 else (0,)
+
+
+def vector_copies(g, u):
+    if g < GRAPHS - 1:
+        return ()
+    return ((0, 0), (1, 0)) if u == ROW_GROUPS - 1 else ((0, 0),)
 
 
 def sum_column(g, b):
@@ -57,7 +67,7 @@ def tile_cheblayer_pa_t_kernel(tc, x, adj, out):
         unread = ctx.enter_context(tc.tile_pool(name="unread", bufs=2))
         row_pool = ctx.enter_context(tc.tile_pool(name="r_row", bufs=2))
         diag_pool = ctx.enter_context(tc.tile_pool(name="diag", bufs=4))
-        x_stage = ctx.enter_context(tc.tile_pool(name="x_stage", bufs=2))
+        x_stage = ctx.enter_context(tc.tile_pool(name="x_stage", bufs=3))
         x_mx = ctx.enter_context(tc.tile_pool(name="x_mx", bufs=2))
         lap_stage = ctx.enter_context(tc.tile_pool(name="lap_stage", bufs=IN_FLIGHT // GROUP))
         lap_mx = ctx.enter_context(tc.tile_pool(name="lap_mx", bufs=IN_FLIGHT // GROUP))
@@ -114,7 +124,7 @@ def tile_cheblayer_pa_t_kernel(tc, x, adj, out):
                         op0=ALU.mult, op1=ALU.add, accum_out=total,
                     )
 
-        def sum_rows_on_tensor(g, u):
+        def fold_rows(g, u):
             folded = turn_psum.tile([P, GROUP, P], F32, tag="turn")
             for k in range(GROUP):
                 for c in range(ROW_BLOCKS):
@@ -125,6 +135,9 @@ def tile_cheblayer_pa_t_kernel(tc, x, adj, out):
                         start=(c == 0),
                         stop=(c == ROW_BLOCKS - 1),
                     )
+            return folded
+
+        def sum_folded(g, u, folded):
             for k in range(GROUP):
                 column = sum_column(g, u * GROUP + k)
                 folded_copy = unread.tile([P, P], F32)
@@ -173,10 +186,10 @@ def tile_cheblayer_pa_t_kernel(tc, x, adj, out):
                 )
             return neg_r, r_row
 
-        def regroup_x(g, q):
+        def regroup_x(g, q, copy):
             s, n = divmod(q, ROW_GROUPS // PASSES)
             grouped = x_stage.tile([P, X_WIDTH, PACK], BF16, align_bytes=64)
-            nc.vector.tensor_copy(
+            copy(
                 out=grouped[:].rearrange("p (c i) t -> p c t i", i=4),
                 in_=x_of[g][:, s, :, n * X_WIDTH : (n + 1) * X_WIDTH].rearrange(
                     "p t (c i) -> p c t i", i=4
@@ -259,32 +272,41 @@ def tile_cheblayer_pa_t_kernel(tc, x, adj, out):
                             start=(s == 0),
                             stop=(s == PASSES - 1),
                         )
-                    nc.scalar.copy(out=result[:, cols], in_=acc[:])
+                    if (b, n) in vector_copies(g, u):
+                        nc.vector.tensor_copy(out=result[:, cols], in_=acc[:])
+                    else:
+                        nc.scalar.copy(out=result[:, cols], in_=acc[:])
                 first_row = (u * GROUP + b) * P
                 nc.sync.dma_start(out=out[g, first_row : first_row + P, :], in_=result[:])
 
+        def x_part_of(step):
+            due = step + X_LEAD
+            return divmod(due, ROW_GROUPS) if 0 <= due < STEPS else None
+
         guess_of, scales_of, x_mx_of = {}, {}, {}
         grouped_of = {}
+        x_grouped_of = {}
         for step in range(-SUM_LEAD, STEPS + 1):
             g, u = divmod(step + SUM_LEAD, ROW_GROUPS)
+            if u == 0 and 0 < g <= GRAPHS:
+                scales_of[g - 1] = refine_scales(g - 1, guess_of[g - 1])
             if g < GRAPHS:
                 if g == 0:
                     sum_rows(g, u)
+                    if u == ROW_GROUPS - 1:
+                        guess_of[g] = guess_scales(g)
                 else:
-                    sum_rows_on_tensor(g, u)
-                if u == ROW_GROUPS - 1:
-                    guess_of[g] = guess_scales(g)
-            if u == 0 and 0 < g <= GRAPHS:
-                scales_of[g - 1] = refine_scales(g - 1, guess_of[g - 1])
+                    folded = fold_rows(g, u)
 
-            x_g, x_q = divmod(step + X_LEAD, ROW_GROUPS)
-            x_due = 0 <= step + X_LEAD < STEPS
-            if x_due:
+            due = x_part_of(step)
+            if due is not None:
+                x_g, x_q = due
                 if x_q == 0:
                     x_codes = x_mx.tile([P, PASSES, FEATURES], U32, align_bytes=64)
                     x_scales = x_mx.tile([P, PASSES, FEATURES], U8, align_bytes=64)
                     x_mx_of[x_g] = (x_codes, x_scales)
-                x_grouped = regroup_x(x_g, x_q)
+                if x_q not in scalar_parts(x_g):
+                    x_grouped_of[due] = regroup_x(x_g, x_q, nc.vector.tensor_copy)
 
             if 0 <= step < STEPS:
                 g, u = divmod(step, ROW_GROUPS)
@@ -292,8 +314,17 @@ def tile_cheblayer_pa_t_kernel(tc, x, adj, out):
                 grouped_of[step] = turn_rows(g, u)
             if 0 <= step - 1:
                 lap_codes, lap_scales = quantise_rows(grouped_of[step - 1])
-            if x_due:
-                quantise_x(x_q, x_grouped, *x_mx_of[x_g])
+            g, u = divmod(step + SUM_LEAD, ROW_GROUPS)
+            if 0 < g < GRAPHS:
+                sum_folded(g, u, folded)
+                if u == ROW_GROUPS - 1:
+                    guess_of[g] = guess_scales(g)
+            if due is not None:
+                quantise_x(x_q, x_grouped_of[due], *x_mx_of[x_g])
             if 0 <= step - 1:
                 g, u = divmod(step - 1, ROW_GROUPS)
                 multiply_and_store(g, u, lap_codes, lap_scales, *x_mx_of[g])
+
+            coming = x_part_of(step + 1)
+            if coming is not None and coming[1] in scalar_parts(coming[0]):
+                x_grouped_of[coming] = regroup_x(*coming, nc.scalar.copy)

@@ -30,9 +30,11 @@ BANK = 512
 FEATURE_TILES = FEATURES // BANK
 X_WIDTH = PASSES * FEATURES // ROW_GROUPS
 
+SUM_LEAD = ROW_GROUPS + 3
+X_TILES = 2 * PASSES
+ADJ_TILES = SUM_LEAD + 4
 LANE = 8
 IN_FLIGHT = 6
-SUM_LEAD = ROW_GROUPS + 3
 X_LEAD = ROW_GROUPS - 1
 
 FLOPS = 2 * GRAPHS * NODES * NODES * FEATURES
@@ -60,8 +62,8 @@ def tile_cheblayer_pa_t_kernel(tc, x, adj, out):
     nc = tc.nc
     with ExitStack() as ctx:
         const = ctx.enter_context(tc.tile_pool(name="const", bufs=1))
-        adj_pool = ctx.enter_context(tc.tile_pool(name="adj", bufs=GRAPHS))
-        x_pool = ctx.enter_context(tc.tile_pool(name="x", bufs=GRAPHS))
+        adj_pool = ctx.enter_context(tc.tile_pool(name="adj", bufs=ADJ_TILES))
+        x_pool = ctx.enter_context(tc.tile_pool(name="x", bufs=X_TILES))
         sum_pool = ctx.enter_context(tc.tile_pool(name="sums", bufs=GRAPHS))
         small = ctx.enter_context(tc.tile_pool(name="small", bufs=2))
         unread = ctx.enter_context(tc.tile_pool(name="unread", bufs=2))
@@ -71,7 +73,7 @@ def tile_cheblayer_pa_t_kernel(tc, x, adj, out):
         x_mx = ctx.enter_context(tc.tile_pool(name="x_mx", bufs=2))
         lap_stage = ctx.enter_context(tc.tile_pool(name="lap_stage", bufs=IN_FLIGHT // GROUP))
         lap_mx = ctx.enter_context(tc.tile_pool(name="lap_mx", bufs=IN_FLIGHT // GROUP))
-        out_pool = ctx.enter_context(tc.tile_pool(name="out", bufs=IN_FLIGHT))
+        out_pool = ctx.enter_context(tc.tile_pool(name="out", bufs=10))
         turn_psum = ctx.enter_context(tc.psum_pool(name="turn", bufs=4))
         acc_psum = ctx.enter_context(tc.psum_pool(name="acc", bufs=4))
 
@@ -85,29 +87,41 @@ def tile_cheblayer_pa_t_kernel(tc, x, adj, out):
         warm = const.tile([P, 1], F32)
         nc.scalar.activation(out=warm[:], in_=eps[:], func=ACT.Abs_reciprocal_sqrt)
 
-        adj_of, x_of, sums_of = [], [], []
+        adj_of, x_of, sums_of = {}, {}, []
         for g in range(GRAPHS):
-            adj_sb = adj_pool.tile([P, ROW_BLOCKS, NODES], BF16)
-            for u in range(ROW_GROUPS):
+            sums = sum_pool.tile([P, 2 * LANE], F32)
+            nc.vector.memset(sums[:], 1.0)
+            sums_of.append(sums)
+
+        def load_rows(n):
+            if n < STEPS:
+                g, u = divmod(n, ROW_GROUPS)
+                rows = adj_pool.tile([P, GROUP, NODES], BF16)
                 nc.sync.dma_start(
-                    out=adj_sb[:, u * GROUP : (u + 1) * GROUP, :],
+                    out=rows[:],
                     in_=adj[g, u * GROUP * P : (u + 1) * GROUP * P, :].rearrange(
                         "(b p) j -> p b j", p=P
                     ),
                 )
-            x_sb = x_pool.tile([P, PASSES, PACK, FEATURES], BF16)
-            for s in range(PASSES):
+                adj_of[n] = rows
+
+        def load_x(n):
+            if n < GRAPHS * PASSES:
+                g, s = divmod(n, PASSES)
+                x_sb = x_pool.tile([P, PACK, FEATURES], BF16)
                 nc.sync.dma_start(
-                    out=x_sb[:, s],
-                    in_=x[g, s * K_PASS : (s + 1) * K_PASS, :].rearrange(
-                        "(p t) f -> p t f", t=PACK
-                    ),
+                    out=x_sb[:],
+                    in_=x[g, s * K_PASS : (s + 1) * K_PASS, :].rearrange("(p t) f -> p t f", t=PACK),
                 )
-            sums = sum_pool.tile([P, 2 * LANE], F32)
-            nc.vector.memset(sums[:], 1.0)
-            adj_of.append(adj_sb)
-            x_of.append(x_sb)
-            sums_of.append(sums)
+                x_of[n] = x_sb
+
+        for g in range(X_TILES // PASSES):
+            for u in range(ROW_GROUPS):
+                load_rows(g * ROW_GROUPS + u)
+            for s in range(PASSES):
+                load_x(g * PASSES + s)
+        for n in range(X_TILES // PASSES * ROW_GROUPS, ADJ_TILES):
+            load_rows(n)
 
         def sum_rows(g, u):
             for b in range(u * GROUP, (u + 1) * GROUP):
@@ -115,12 +129,12 @@ def tile_cheblayer_pa_t_kernel(tc, x, adj, out):
                 if b < scalar_sums(g):
                     scalar_copy = unread.tile([P, NODES], BF16)
                     nc.scalar.activation(
-                        out=scalar_copy[:], in_=adj_of[g][:, b, :], func=ACT.Copy, accum_out=total
+                        out=scalar_copy[:], in_=adj_of[g * ROW_GROUPS + u][:, b - u * GROUP, :], func=ACT.Copy, accum_out=total
                     )
                 else:
                     vector_copy = unread.tile([P, NODES], BF16)
                     nc.vector.tensor_scalar(
-                        out=vector_copy[:], in0=adj_of[g][:, b, :], scalar1=1.0, scalar2=None,
+                        out=vector_copy[:], in0=adj_of[g * ROW_GROUPS + u][:, b - u * GROUP, :], scalar1=1.0, scalar2=None,
                         op0=ALU.mult, op1=ALU.add, accum_out=total,
                     )
 
@@ -131,7 +145,7 @@ def tile_cheblayer_pa_t_kernel(tc, x, adj, out):
                     nc.tensor.matmul(
                         out=folded[:, k, :],
                         lhsT=ident_bf16[:],
-                        rhs=adj_of[g][:, u * GROUP + k, c * P : (c + 1) * P],
+                        rhs=adj_of[g * ROW_GROUPS + u][:, k, c * P : (c + 1) * P],
                         start=(c == 0),
                         stop=(c == ROW_BLOCKS - 1),
                     )
@@ -191,7 +205,7 @@ def tile_cheblayer_pa_t_kernel(tc, x, adj, out):
             grouped = x_stage.tile([P, X_WIDTH, PACK], BF16, align_bytes=64)
             copy(
                 out=grouped[:].rearrange("p (c i) t -> p c t i", i=4),
-                in_=x_of[g][:, s, :, n * X_WIDTH : (n + 1) * X_WIDTH].rearrange(
+                in_=x_of[g * PASSES + s][:, :, n * X_WIDTH : (n + 1) * X_WIDTH].rearrange(
                     "p t (c i) -> p c t i", i=4
                 ),
             )
@@ -207,13 +221,13 @@ def tile_cheblayer_pa_t_kernel(tc, x, adj, out):
             )
 
         def form_rows(g, u, neg_r, r_row):
-            adj_sb = adj_of[g]
+            rows = adj_of[g * ROW_GROUPS + u]
             blocks = range(u * GROUP, (u + 1) * GROUP)
             products = {}
             for b in blocks:
                 product = diag_pool.tile([P, P], F32)
                 nc.vector.scalar_tensor_tensor(
-                    out=product[:], in0=adj_sb[:, b, b * P : (b + 1) * P],
+                    out=product[:], in0=rows[:, b - u * GROUP, b * P : (b + 1) * P],
                     scalar=neg_r[:, sum_column(g, b) : sum_column(g, b) + 1],
                     in1=r_row[:, b * P : (b + 1) * P], op0=ALU.mult, op1=ALU.mult,
                 )
@@ -222,16 +236,16 @@ def tile_cheblayer_pa_t_kernel(tc, x, adj, out):
                 for lo, hi in ((0, b * P), ((b + 1) * P, NODES)):
                     if lo < hi:
                         nc.vector.scalar_tensor_tensor(
-                            out=adj_sb[:, b, lo:hi], in0=adj_sb[:, b, lo:hi],
+                            out=rows[:, b - u * GROUP, lo:hi], in0=rows[:, b - u * GROUP, lo:hi],
                             scalar=neg_r[:, sum_column(g, b) : sum_column(g, b) + 1],
                             in1=r_row[:, lo:hi], op0=ALU.mult, op1=ALU.mult,
                         )
                 nc.vector.tensor_add(
-                    out=adj_sb[:, b, b * P : (b + 1) * P], in0=products[b][:], in1=ident[:]
+                    out=rows[:, b - u * GROUP, b * P : (b + 1) * P], in0=products[b][:], in1=ident[:]
                 )
 
         def turn_rows(g, u):
-            words = adj_of[g][:].bitcast(F32).rearrange(
+            words = adj_of[g * ROW_GROUPS + u][:].bitcast(F32).rearrange(
                 "p b (s w h) -> p b s h w", s=PASSES, h=HALVES
             )
             grouped = lap_stage.tile([P, GROUP, PASSES, P, HALVES], F32, align_bytes=64)
@@ -240,7 +254,7 @@ def tile_cheblayer_pa_t_kernel(tc, x, adj, out):
                 for s in range(PASSES):
                     for h in range(HALVES):
                         nc.tensor.transpose(
-                            turned[:, s, h, :], words[:, u * GROUP + b, s, h, :], ident[:]
+                            turned[:, s, h, :], words[:, b, s, h, :], ident[:]
                         )
                 nc.scalar.copy(out=grouped[:, b], in_=turned[:].rearrange("p s h m -> p s m h"))
             return grouped
@@ -328,3 +342,8 @@ def tile_cheblayer_pa_t_kernel(tc, x, adj, out):
             coming = x_part_of(step + 1)
             if coming is not None and coming[1] in scalar_parts(coming[0]):
                 x_grouped_of[coming] = regroup_x(*coming, nc.scalar.copy)
+
+            if 0 <= step:
+                load_rows(step + ADJ_TILES)
+            if due is not None and x_q % 2 == 1:
+                load_x(x_g * PASSES + x_q // 2 + X_TILES)

@@ -28,34 +28,29 @@ ROW_GROUPS = ROW_BLOCKS // GROUP
 STEPS = GRAPHS * ROW_GROUPS
 BANK = 512
 FEATURE_TILES = FEATURES // BANK
-X_WIDTH = PASSES * FEATURES // ROW_GROUPS
 
-SUM_LEAD = ROW_GROUPS + 3
 X_TILES = 2 * PASSES
-ADJ_TILES = SUM_LEAD + 4
+FOLD = 64
+PARTS = 4
+PARTS_PER_PASS = PARTS // PASSES
+X_WIDTH = FEATURES // PARTS_PER_PASS
+S_COLUMNS = 160
+HEAD_COLUMNS = {0: 0, 1: X_WIDTH, 2: X_WIDTH, 3: X_WIDTH}
+X_LEAD = PARTS - 1
+FOLD_LEAD = ROW_GROUPS + 3
+ADJ_TILES = 12
 LANE = 8
 IN_FLIGHT = 6
-X_LEAD = ROW_GROUPS - 1
 
 FLOPS = 2 * GRAPHS * NODES * NODES * FEATURES
 
 
-def scalar_sums(g):
-    return ROW_BLOCKS // 2 if g == 0 else ROW_BLOCKS
-
-
-def scalar_parts(g):
-    return (0, 2) if g == 0 else (0,)
-
-
-def vector_copies(g, u):
-    if g < GRAPHS - 1:
-        return ()
-    return ((0, 0), (1, 0)) if u == ROW_GROUPS - 1 else ((0, 0),)
+def scalar_columns(m):
+    return HEAD_COLUMNS.get(m, S_COLUMNS)
 
 
 def sum_column(g, b):
-    return b if b < scalar_sums(g) else LANE + b - scalar_sums(g)
+    return b if g > 0 else b // 2 + LANE * (b % 2)
 
 
 def tile_cheblayer_pa_t_kernel(tc, x, adj, out):
@@ -69,13 +64,16 @@ def tile_cheblayer_pa_t_kernel(tc, x, adj, out):
         unread = ctx.enter_context(tc.tile_pool(name="unread", bufs=2))
         row_pool = ctx.enter_context(tc.tile_pool(name="r_row", bufs=2))
         diag_pool = ctx.enter_context(tc.tile_pool(name="diag", bufs=4))
-        x_stage = ctx.enter_context(tc.tile_pool(name="x_stage", bufs=3))
+        x_stage = ctx.enter_context(tc.tile_pool(name="x_stage", bufs=5))
         x_mx = ctx.enter_context(tc.tile_pool(name="x_mx", bufs=2))
         lap_stage = ctx.enter_context(tc.tile_pool(name="lap_stage", bufs=IN_FLIGHT // GROUP))
         lap_mx = ctx.enter_context(tc.tile_pool(name="lap_mx", bufs=IN_FLIGHT // GROUP))
         out_pool = ctx.enter_context(tc.tile_pool(name="out", bufs=10))
-        turn_psum = ctx.enter_context(tc.psum_pool(name="turn", bufs=4))
+        turn_psum = ctx.enter_context(tc.psum_pool(name="turn", bufs=3))
+        fold_psum = ctx.enter_context(tc.psum_pool(name="fold", bufs=1))
         acc_psum = ctx.enter_context(tc.psum_pool(name="acc", bufs=4))
+
+        ctx.enter_context(tc.manual_schedule())
 
         ident = const.tile([P, P], F32)
         make_identity(nc, ident[:])
@@ -115,50 +113,40 @@ def tile_cheblayer_pa_t_kernel(tc, x, adj, out):
                 )
                 x_of[n] = x_sb
 
-        for g in range(X_TILES // PASSES):
-            for u in range(ROW_GROUPS):
-                load_rows(g * ROW_GROUPS + u)
-            for s in range(PASSES):
-                load_x(g * PASSES + s)
-        for n in range(X_TILES // PASSES * ROW_GROUPS, ADJ_TILES):
-            load_rows(n)
-
-        def sum_rows(g, u):
-            for b in range(u * GROUP, (u + 1) * GROUP):
-                total = sums_of[g][:, sum_column(g, b) : sum_column(g, b) + 1]
-                if b < scalar_sums(g):
+        def sum_rows(u):
+            for k in range(GROUP):
+                column = sum_column(0, u * GROUP + k)
+                total = sums_of[0][:, column : column + 1]
+                if k == 0:
                     scalar_copy = unread.tile([P, NODES], BF16)
                     nc.scalar.activation(
-                        out=scalar_copy[:], in_=adj_of[g * ROW_GROUPS + u][:, b - u * GROUP, :], func=ACT.Copy, accum_out=total
+                        out=scalar_copy[:], in_=adj_of[u][:, k, :], func=ACT.Copy, accum_out=total
                     )
                 else:
                     vector_copy = unread.tile([P, NODES], BF16)
                     nc.vector.tensor_scalar(
-                        out=vector_copy[:], in0=adj_of[g * ROW_GROUPS + u][:, b - u * GROUP, :], scalar1=1.0, scalar2=None,
+                        out=vector_copy[:], in0=adj_of[u][:, k, :], scalar1=1.0, scalar2=None,
                         op0=ALU.mult, op1=ALU.add, accum_out=total,
                     )
 
         def fold_rows(g, u):
-            folded = turn_psum.tile([P, GROUP, P], F32, tag="turn")
+            if u == 0:
+                folded_of[g] = fold_psum.tile([P, ROW_BLOCKS, FOLD], F32, name="folded")
             for k in range(GROUP):
-                for c in range(ROW_BLOCKS):
+                for c in range(NODES // FOLD):
                     nc.tensor.matmul(
-                        out=folded[:, k, :],
+                        out=folded_of[g][:, u * GROUP + k, :],
                         lhsT=ident_bf16[:],
-                        rhs=adj_of[g * ROW_GROUPS + u][:, k, c * P : (c + 1) * P],
+                        rhs=adj_of[g * ROW_GROUPS + u][:, k, c * FOLD : (c + 1) * FOLD],
                         start=(c == 0),
-                        stop=(c == ROW_BLOCKS - 1),
+                        stop=(c == NODES // FOLD - 1),
                     )
-            return folded
 
-        def sum_folded(g, u, folded):
-            for k in range(GROUP):
-                column = sum_column(g, u * GROUP + k)
-                folded_copy = unread.tile([P, P], F32)
-                nc.scalar.activation(
-                    out=folded_copy[:], in_=folded[:, k, :], func=ACT.Copy,
-                    accum_out=sums_of[g][:, column : column + 1],
-                )
+        def sum_folded(g):
+            nc.vector.tensor_reduce(
+                out=sums_of[g][:, :ROW_BLOCKS], in_=folded_of[g][:],
+                axis=mybir.AxisListType.X, op=ALU.add,
+            )
 
         def guess_scales(g):
             guess = small.tile([P, 2 * LANE], F32)
@@ -182,8 +170,11 @@ def tile_cheblayer_pa_t_kernel(tc, x, adj, out):
                 out=neg_r[:], in0=near_half[:], scalar=1.5, in1=guess[:],
                 op0=ALU.subtract, op1=ALU.mult,
             )
-            r_row = row_pool.tile([P, NODES], F32)
+            return neg_r
+
+        def spread_scales(g, neg_r):
             blocks_per_bank = BANK // P
+            spreads = []
             for h in range(NODES // BANK):
                 spread = turn_psum.tile([P, blocks_per_bank, P], F32, tag="turn")
                 for q in range(blocks_per_bank):
@@ -193,157 +184,247 @@ def tile_cheblayer_pa_t_kernel(tc, x, adj, out):
                         neg_r[:, column : column + 1].to_broadcast([P, P]),
                         ident[:],
                     )
-                nc.scalar.mul(
-                    out=r_row[:, h * BANK : (h + 1) * BANK],
-                    in_=spread[:].rearrange("p q n -> p (q n)"),
-                    mul=-1.0,
-                )
-            return neg_r, r_row
+                spreads.append(spread)
+            return spreads
 
-        def regroup_x(g, q, copy):
-            s, n = divmod(q, ROW_GROUPS // PASSES)
-            grouped = x_stage.tile([P, X_WIDTH, PACK], BF16, align_bytes=64)
+        def copy_scales(g, spreads):
+            r_row = row_pool.tile([P, NODES], F32)
+            for h, spread in enumerate(spreads):
+                to = r_row[:, h * BANK : (h + 1) * BANK]
+                source = spread[:].rearrange("p q n -> p (q n)")
+                if g == 0:
+                    nc.vector.tensor_scalar_mul(out=to, in0=source, scalar1=-1.0)
+                else:
+                    nc.scalar.mul(out=to, in_=source, mul=-1.0)
+            return r_row
+
+        def lay_out(m, engine, half=None):
+            if m >= GRAPHS * PARTS:
+                return
+            mid = X_WIDTH - scalar_columns(m)
+            lo, hi = (mid, X_WIDTH) if engine == "scalar" else (0, mid)
+            if half is not None:
+                cut = lo + (hi - lo) // 2 // 16 * 16
+                lo, hi = ((lo, cut), (cut, hi))[half]
+            if lo == hi:
+                return
+            g, q = divmod(m, PARTS)
+            s, n = divmod(q, PARTS_PER_PASS)
+            if m not in x_grouped_of:
+                x_grouped_of[m] = x_stage.tile(
+                    [P, X_WIDTH, PACK], BF16, align_bytes=64, name="grouped"
+                )
+            copy = nc.scalar.copy if engine == "scalar" else nc.vector.tensor_copy
             copy(
-                out=grouped[:].rearrange("p (c i) t -> p c t i", i=4),
-                in_=x_of[g * PASSES + s][:, :, n * X_WIDTH : (n + 1) * X_WIDTH].rearrange(
+                out=x_grouped_of[m][:, lo:hi].rearrange("p (c i) t -> p c t i", i=4),
+                in_=x_of[g * PASSES + s][:, :, n * X_WIDTH + lo : n * X_WIDTH + hi].rearrange(
                     "p t (c i) -> p c t i", i=4
                 ),
             )
-            return grouped
 
-        def quantise_x(q, grouped, x_codes, x_scales):
-            s, n = divmod(q, ROW_GROUPS // PASSES)
+        def quantise_part(m):
+            if m >= GRAPHS * PARTS:
+                return
+            g, q = divmod(m, PARTS)
+            s, n = divmod(q, PARTS_PER_PASS)
+            if q == 0:
+                x_codes = x_mx.tile([P, PASSES, FEATURES], U32, align_bytes=64)
+                x_scales = x_mx.tile([P, PASSES, FEATURES], U8, align_bytes=64)
+                x_mx_of[g] = (x_codes, x_scales)
+            x_codes, x_scales = x_mx_of[g]
             cols = slice(n * X_WIDTH, (n + 1) * X_WIDTH)
             nc.vector.quantize_mx(
                 out=x_codes[:, s, cols].bitcast(FP8X4),
                 scales=x_scales[:, s, cols],
-                in_=grouped[:].rearrange("p f t -> p (f t)"),
+                in_=x_grouped_of[m][:].rearrange("p f t -> p (f t)"),
             )
 
-        def form_rows(g, u, neg_r, r_row):
-            rows = adj_of[g * ROW_GROUPS + u]
-            blocks = range(u * GROUP, (u + 1) * GROUP)
-            products = {}
-            for b in blocks:
+        def form_products(n):
+            g, u = divmod(n, ROW_GROUPS)
+            neg_r, r_row = scales_of[g]
+            products_of[n] = []
+            for k in range(GROUP):
+                b = u * GROUP + k
                 product = diag_pool.tile([P, P], F32)
                 nc.vector.scalar_tensor_tensor(
-                    out=product[:], in0=rows[:, b - u * GROUP, b * P : (b + 1) * P],
+                    out=product[:], in0=adj_of[n][:, k, b * P : (b + 1) * P],
                     scalar=neg_r[:, sum_column(g, b) : sum_column(g, b) + 1],
                     in1=r_row[:, b * P : (b + 1) * P], op0=ALU.mult, op1=ALU.mult,
                 )
-                products[b] = product
-            for b in blocks:
-                for lo, hi in ((0, b * P), ((b + 1) * P, NODES)):
-                    if lo < hi:
-                        nc.vector.scalar_tensor_tensor(
-                            out=rows[:, b - u * GROUP, lo:hi], in0=rows[:, b - u * GROUP, lo:hi],
-                            scalar=neg_r[:, sum_column(g, b) : sum_column(g, b) + 1],
-                            in1=r_row[:, lo:hi], op0=ALU.mult, op1=ALU.mult,
-                        )
-                nc.vector.tensor_add(
-                    out=rows[:, b - u * GROUP, b * P : (b + 1) * P], in0=products[b][:], in1=ident[:]
-                )
+                products_of[n].append(product)
 
-        def turn_rows(g, u):
-            words = adj_of[g * ROW_GROUPS + u][:].bitcast(F32).rearrange(
+        def form_block(n, k):
+            g, u = divmod(n, ROW_GROUPS)
+            neg_r, r_row = scales_of[g]
+            b = u * GROUP + k
+            row = adj_of[n][:, k, :]
+            for lo, hi in ((0, b * P), ((b + 1) * P, NODES)):
+                if lo < hi:
+                    nc.vector.scalar_tensor_tensor(
+                        out=row[:, lo:hi], in0=row[:, lo:hi],
+                        scalar=neg_r[:, sum_column(g, b) : sum_column(g, b) + 1],
+                        in1=r_row[:, lo:hi], op0=ALU.mult, op1=ALU.mult,
+                    )
+            nc.vector.tensor_add(
+                out=row[:, b * P : (b + 1) * P], in0=products_of[n][k][:], in1=ident[:]
+            )
+
+        def turn_block(n, k):
+            words = adj_of[n][:].bitcast(F32).rearrange(
                 "p b (s w h) -> p b s h w", s=PASSES, h=HALVES
             )
-            grouped = lap_stage.tile([P, GROUP, PASSES, P, HALVES], F32, align_bytes=64)
-            for b in range(GROUP):
-                turned = turn_psum.tile([P, PASSES, HALVES, P], F32, tag="turn")
-                for s in range(PASSES):
-                    for h in range(HALVES):
-                        nc.tensor.transpose(
-                            turned[:, s, h, :], words[:, b, s, h, :], ident[:]
-                        )
-                nc.scalar.copy(out=grouped[:, b], in_=turned[:].rearrange("p s h m -> p s m h"))
-            return grouped
+            if k == 0:
+                turned_of[n] = lap_stage.tile(
+                    [P, GROUP, PASSES, P, HALVES], F32, align_bytes=64, name="turned_rows"
+                )
+            turned = turn_psum.tile([P, PASSES, HALVES, P], F32, tag="turn")
+            for s in range(PASSES):
+                for h in range(HALVES):
+                    nc.tensor.transpose(turned[:, s, h, :], words[:, k, s, h, :], ident[:])
+            bank_of[n, k] = turned
 
-        def quantise_rows(grouped):
-            lap_codes = lap_mx.tile([P, GROUP * PASSES * P], U32, align_bytes=64)
-            lap_scales = lap_mx.tile([P, GROUP * PASSES * P], U8, align_bytes=64)
+        def move_turned(n, k, copy):
+            copy(out=turned_of[n][:, k], in_=bank_of[n, k][:].rearrange("p s h m -> p s m h"))
+
+        def quantise_blocks(n, first, last):
+            width = (last + 1 - first) * PASSES * P
+            codes = lap_mx.tile([P, width], U32, align_bytes=64, tag=f"codes{width}")
+            scales = lap_mx.tile([P, width], U8, align_bytes=64, tag=f"scales{width}")
             nc.vector.quantize_mx(
-                out=lap_codes[:].bitcast(FP8X4),
-                scales=lap_scales[:],
-                in_=grouped[:].rearrange("p b s m h -> p (b s m h)").bitcast(BF16),
+                out=codes[:].bitcast(FP8X4),
+                scales=scales[:],
+                in_=turned_of[n][:, first : last + 1]
+                .rearrange("p b s m h -> p (b s m h)")
+                .bitcast(BF16),
             )
-            return lap_codes, lap_scales
+            for k in range(first, last + 1):
+                mine = slice((k - first) * PASSES * P, (k + 1 - first) * PASSES * P)
+                lap_of[n, k] = (codes[:, mine], scales[:, mine])
 
-        def multiply_and_store(g, u, lap_codes, lap_scales, x_codes, x_scales):
-            for b in range(GROUP):
-                result = out_pool.tile([P, FEATURES], F32)
-                for n in range(FEATURE_TILES):
-                    cols = slice(n * BANK, (n + 1) * BANK)
-                    acc = acc_psum.tile([P, BANK], F32)
-                    for s in range(PASSES):
-                        rows = slice((b * PASSES + s) * P, (b * PASSES + s + 1) * P)
-                        nc.tensor.matmul_mx(
-                            out=acc[:],
-                            lhsT=lap_codes[:, rows].bitcast(FP8X4),
-                            lhsT_scale=lap_scales[:, rows],
-                            rhs=x_codes[:, s, cols].bitcast(FP8X4),
-                            rhs_scale=x_scales[:, s, cols],
-                            start=(s == 0),
-                            stop=(s == PASSES - 1),
-                        )
-                    if (b, n) in vector_copies(g, u):
-                        nc.vector.tensor_copy(out=result[:, cols], in_=acc[:])
-                    else:
-                        nc.scalar.copy(out=result[:, cols], in_=acc[:])
-                first_row = (u * GROUP + b) * P
+        def multiply_block(n, k):
+            codes, scales = lap_of[n, k]
+            x_codes, x_scales = x_mx_of[n // ROW_GROUPS]
+            acc_of[n, k] = []
+            for f in range(FEATURE_TILES):
+                cols = slice(f * BANK, (f + 1) * BANK)
+                acc = acc_psum.tile([P, BANK], F32)
+                for s in range(PASSES):
+                    nc.tensor.matmul_mx(
+                        out=acc[:],
+                        lhsT=codes[:, s * P : (s + 1) * P].bitcast(FP8X4),
+                        lhsT_scale=scales[:, s * P : (s + 1) * P],
+                        rhs=x_codes[:, s, cols].bitcast(FP8X4),
+                        rhs_scale=x_scales[:, s, cols],
+                        start=(s == 0),
+                        stop=(s == PASSES - 1),
+                    )
+                acc_of[n, k].append(acc)
+
+        def copy_result(n, k, f, copy):
+            if (n, k) not in result_of:
+                result_of[n, k] = out_pool.tile([P, FEATURES], F32, name="result")
+                left_of[n, k] = FEATURE_TILES
+            result = result_of[n, k]
+            copy(out=result[:, f * BANK : (f + 1) * BANK], in_=acc_of[n, k][f][:])
+            left_of[n, k] -= 1
+            if left_of[n, k] == 0:
+                g, u = divmod(n, ROW_GROUPS)
+                first_row = (u * GROUP + k) * P
                 nc.sync.dma_start(out=out[g, first_row : first_row + P, :], in_=result[:])
 
-        def x_part_of(step):
-            due = step + X_LEAD
-            return divmod(due, ROW_GROUPS) if 0 <= due < STEPS else None
-
-        guess_of, scales_of, x_mx_of = {}, {}, {}
-        grouped_of = {}
+        folded_of, x_mx_of, scales_of = {}, {}, {}
         x_grouped_of = {}
-        for step in range(-SUM_LEAD, STEPS + 1):
-            g, u = divmod(step + SUM_LEAD, ROW_GROUPS)
-            if u == 0 and 0 < g <= GRAPHS:
-                scales_of[g - 1] = refine_scales(g - 1, guess_of[g - 1])
-            if g < GRAPHS:
-                if g == 0:
-                    sum_rows(g, u)
-                    if u == ROW_GROUPS - 1:
-                        guess_of[g] = guess_scales(g)
-                else:
-                    folded = fold_rows(g, u)
+        products_of, turned_of = {}, {}
+        bank_of, lap_of, acc_of, result_of, left_of = {}, {}, {}, {}, {}
+        on_scalar, on_vector = nc.scalar.copy, nc.vector.tensor_copy
 
-            due = x_part_of(step)
-            if due is not None:
-                x_g, x_q = due
-                if x_q == 0:
-                    x_codes = x_mx.tile([P, PASSES, FEATURES], U32, align_bytes=64)
-                    x_scales = x_mx.tile([P, PASSES, FEATURES], U8, align_bytes=64)
-                    x_mx_of[x_g] = (x_codes, x_scales)
-                if x_q not in scalar_parts(x_g):
-                    x_grouped_of[due] = regroup_x(x_g, x_q, nc.vector.tensor_copy)
+        for n in range(ROW_GROUPS):
+            load_rows(n)
+        for n in range(PASSES):
+            load_x(n)
+        load_rows(ROW_GROUPS)
+        load_rows(ROW_GROUPS + 1)
+        load_x(PASSES)
+        for n in range(ROW_GROUPS + 2, 2 * ROW_GROUPS):
+            load_rows(n)
+        load_x(PASSES + 1)
+        for n in range(2 * ROW_GROUPS, ADJ_TILES):
+            load_rows(n)
 
-            if 0 <= step < STEPS:
-                g, u = divmod(step, ROW_GROUPS)
-                form_rows(g, u, *scales_of[g])
-                grouped_of[step] = turn_rows(g, u)
-            if 0 <= step - 1:
-                lap_codes, lap_scales = quantise_rows(grouped_of[step - 1])
-            g, u = divmod(step + SUM_LEAD, ROW_GROUPS)
-            if 0 < g < GRAPHS:
-                sum_folded(g, u, folded)
-                if u == ROW_GROUPS - 1:
-                    guess_of[g] = guess_scales(g)
-            if due is not None:
-                quantise_x(x_q, x_grouped_of[due], *x_mx_of[x_g])
-            if 0 <= step - 1:
-                g, u = divmod(step - 1, ROW_GROUPS)
-                multiply_and_store(g, u, lap_codes, lap_scales, *x_mx_of[g])
+        for u in range(ROW_GROUPS):
+            sum_rows(u)
+        guess = guess_scales(0)
+        neg_r = refine_scales(0, guess)
+        spreads = spread_scales(0, neg_r)
+        lay_out(0, "vector")
+        for m in range(PARTS):
+            lay_out(m, "scalar")
+        scales_of[0] = (neg_r, copy_scales(0, spreads))
+        fold_rows(1, 0)
 
-            coming = x_part_of(step + 1)
-            if coming is not None and coming[1] in scalar_parts(coming[0]):
-                x_grouped_of[coming] = regroup_x(*coming, nc.scalar.copy)
+        load_x(X_TILES)
 
-            if 0 <= step:
-                load_rows(step + ADJ_TILES)
-            if due is not None and x_q % 2 == 1:
-                load_x(x_g * PASSES + x_q // 2 + X_TILES)
+        for step in range(STEPS):
+            fold_g, fold_u = divmod(step + FOLD_LEAD, ROW_GROUPS)
+            due_g, due = divmod(step + 3, ROW_GROUPS)
+            due_g = due_g if 1 <= due_g < GRAPHS else 0
+            final = step == STEPS - 1
+
+            form_products(step)
+            form_block(step, 0)
+            turn_block(step, 0)
+            move_turned(step, 0, on_scalar)
+            if due_g and due == 1:
+                guess = guess_scales(due_g)
+            if due_g and due == 2:
+                spreads = spread_scales(due_g, neg_r)
+            if due_g and due == 2:
+                scales_of[due_g] = (neg_r, copy_scales(due_g, spreads))
+            lay_out(step + X_LEAD + 1, "scalar")
+            form_block(step, 1)
+            turn_block(step, 1)
+            move_turned(step, 1, on_scalar)
+            if step > 0:
+                quantise_blocks(step - 1, 0, GROUP - 1)
+            if step > 0:
+                multiply_block(step - 1, 0)
+            if step > 0:
+                copy_result(step - 1, 0, 0, on_scalar)
+            if step > 0 and not final:
+                copy_result(step - 1, 0, 1, on_scalar)
+            if step > 0:
+                multiply_block(step - 1, 1)
+            if step > 0:
+                copy_result(step - 1, 1, 0, on_scalar)
+            if final:
+                copy_result(step - 1, 0, 1, on_vector)
+            if step > 0 and not final:
+                copy_result(step - 1, 1, 1, on_scalar)
+            if step == 0:
+                quantise_part(0)
+                lay_out(3, "vector")
+                quantise_part(1)
+                quantise_part(2)
+            quantise_part(step + X_LEAD)
+            if due_g and due == 0:
+                sum_folded(due_g)
+            lay_out(step + X_LEAD + 1, "vector")
+            if due_g and due == 1:
+                neg_r = refine_scales(due_g, guess)
+            if step == 0:
+                for u in range(1, ROW_GROUPS):
+                    fold_rows(1, u)
+            elif fold_g < GRAPHS:
+                fold_rows(fold_g, fold_u)
+            load_rows(step + ADJ_TILES)
+            if (step + X_LEAD) % 2 == 1:
+                load_x((step + X_LEAD) // 2 + X_TILES)
+
+        n = STEPS - 1
+        quantise_blocks(n, 0, 0)
+        quantise_blocks(n, 1, 1)
+        copy_result(n - 1, 1, 1, on_vector)
+        for k in range(GROUP):
+            multiply_block(n, k)
+            copy_result(n, k, 0, on_scalar)
+            copy_result(n, k, 1, on_vector)

@@ -34,7 +34,8 @@ FOLD = 64
 PARTS = 4
 PARTS_PER_PASS = PARTS // PASSES
 X_WIDTH = FEATURES // PARTS_PER_PASS
-S_COLUMNS = 160
+DIAGONAL_STEP = NODES + P
+S_COLUMNS = 240
 HEAD_COLUMNS = {0: 0, 1: X_WIDTH, 2: X_WIDTH, 3: X_WIDTH}
 X_LEAD = PARTS - 1
 FOLD_LEAD = ROW_GROUPS + 3
@@ -63,7 +64,7 @@ def tile_cheblayer_pa_t_kernel(tc, x, adj, out):
         small = ctx.enter_context(tc.tile_pool(name="small", bufs=2))
         unread = ctx.enter_context(tc.tile_pool(name="unread", bufs=2))
         row_pool = ctx.enter_context(tc.tile_pool(name="r_row", bufs=2))
-        diag_pool = ctx.enter_context(tc.tile_pool(name="diag", bufs=4))
+        diag_pool = ctx.enter_context(tc.tile_pool(name="diag", bufs=2))
         x_stage = ctx.enter_context(tc.tile_pool(name="x_stage", bufs=5))
         x_mx = ctx.enter_context(tc.tile_pool(name="x_mx", bufs=2))
         lap_stage = ctx.enter_context(tc.tile_pool(name="lap_stage", bufs=IN_FLIGHT // GROUP))
@@ -85,7 +86,8 @@ def tile_cheblayer_pa_t_kernel(tc, x, adj, out):
         warm = const.tile([P, 1], F32)
         nc.scalar.activation(out=warm[:], in_=eps[:], func=ACT.Abs_reciprocal_sqrt)
 
-        adj_of, x_of, sums_of = {}, {}, []
+        adj_of, diagonal_of = {}, {}
+        x_of, sums_of = {}, []
         for g in range(GRAPHS):
             sums = sum_pool.tile([P, 2 * LANE], F32)
             nc.vector.memset(sums[:], 1.0)
@@ -94,14 +96,19 @@ def tile_cheblayer_pa_t_kernel(tc, x, adj, out):
         def load_rows(n):
             if n < STEPS:
                 g, u = divmod(n, ROW_GROUPS)
-                rows = adj_pool.tile([P, GROUP, NODES], BF16)
+                flat = adj_pool.tile([P, GROUP * DIAGONAL_STEP], BF16)
+                rows = flat[:, : GROUP * NODES].rearrange("p (k j) -> p k j", k=GROUP)
                 nc.sync.dma_start(
-                    out=rows[:],
+                    out=rows,
                     in_=adj[g, u * GROUP * P : (u + 1) * GROUP * P, :].rearrange(
                         "(b p) j -> p b j", p=P
                     ),
                 )
                 adj_of[n] = rows
+                first = u * GROUP * P
+                diagonal_of[n] = flat[:].rearrange("p (k y) -> p k y", k=GROUP)[
+                    :, :, first : first + P
+                ]
 
         def load_x(n):
             if n < GRAPHS * PASSES:
@@ -241,17 +248,15 @@ def tile_cheblayer_pa_t_kernel(tc, x, adj, out):
 
         def form_products(n):
             g, u = divmod(n, ROW_GROUPS)
-            neg_r, r_row = scales_of[g]
-            products_of[n] = []
-            for k in range(GROUP):
-                b = u * GROUP + k
-                product = diag_pool.tile([P, P], F32)
-                nc.vector.scalar_tensor_tensor(
-                    out=product[:], in0=adj_of[n][:, k, b * P : (b + 1) * P],
-                    scalar=neg_r[:, sum_column(g, b) : sum_column(g, b) + 1],
-                    in1=r_row[:, b * P : (b + 1) * P], op0=ALU.mult, op1=ALU.mult,
-                )
-                products_of[n].append(product)
+            products_of[n] = diag_pool.tile([P, GROUP, P], F32, name="products")
+            nc.vector.tensor_tensor(
+                out=products_of[n][:],
+                in0=diagonal_of[n],
+                in1=scales_of[g][1][:, u * GROUP * P : (u + 1) * GROUP * P].rearrange(
+                    "p (k j) -> p k j", k=GROUP
+                ),
+                op=ALU.mult,
+            )
 
         def form_block(n, k):
             g, u = divmod(n, ROW_GROUPS)
@@ -265,8 +270,10 @@ def tile_cheblayer_pa_t_kernel(tc, x, adj, out):
                         scalar=neg_r[:, sum_column(g, b) : sum_column(g, b) + 1],
                         in1=r_row[:, lo:hi], op0=ALU.mult, op1=ALU.mult,
                     )
-            nc.vector.tensor_add(
-                out=row[:, b * P : (b + 1) * P], in0=products_of[n][k][:], in1=ident[:]
+            nc.vector.scalar_tensor_tensor(
+                out=row[:, b * P : (b + 1) * P], in0=products_of[n][:, k, :],
+                scalar=neg_r[:, sum_column(g, b) : sum_column(g, b) + 1],
+                in1=ident[:], op0=ALU.mult, op1=ALU.add,
             )
 
         def turn_block(n, k):
@@ -396,8 +403,6 @@ def tile_cheblayer_pa_t_kernel(tc, x, adj, out):
                 multiply_block(step - 1, 1)
             if step > 0:
                 copy_result(step - 1, 1, 0, on_scalar)
-            if final:
-                copy_result(step - 1, 0, 1, on_vector)
             if step > 0 and not final:
                 copy_result(step - 1, 1, 1, on_scalar)
             if step == 0:
@@ -422,6 +427,7 @@ def tile_cheblayer_pa_t_kernel(tc, x, adj, out):
 
         n = STEPS - 1
         quantise_blocks(n, 0, 0)
+        copy_result(n - 1, 0, 1, on_vector)
         quantise_blocks(n, 1, 1)
         copy_result(n - 1, 1, 1, on_vector)
         for k in range(GROUP):

@@ -35,7 +35,7 @@ PARTS = 4
 PARTS_PER_PASS = PARTS // PASSES
 X_WIDTH = FEATURES // PARTS_PER_PASS
 DIAGONAL_STEP = NODES + P
-S_COLUMNS = 240
+S_COLUMNS = 208
 HEAD_COLUMNS = {0: 0, 1: X_WIDTH, 2: X_WIDTH, 3: X_WIDTH}
 X_LEAD = PARTS - 1
 FOLD_LEAD = ROW_GROUPS + 3
@@ -139,15 +139,14 @@ def tile_cheblayer_pa_t_kernel(tc, x, adj, out):
         def fold_rows(g, u):
             if u == 0:
                 folded_of[g] = fold_psum.tile([P, ROW_BLOCKS, FOLD], F32, name="folded")
-            for k in range(GROUP):
-                for c in range(NODES // FOLD):
-                    nc.tensor.matmul(
-                        out=folded_of[g][:, u * GROUP + k, :],
-                        lhsT=ident_bf16[:],
-                        rhs=adj_of[g * ROW_GROUPS + u][:, k, c * FOLD : (c + 1) * FOLD],
-                        start=(c == 0),
-                        stop=(c == NODES // FOLD - 1),
-                    )
+            for c in range(NODES // FOLD):
+                nc.tensor.matmul(
+                    out=folded_of[g][:, u * GROUP : (u + 1) * GROUP, :],
+                    lhsT=ident_bf16[:],
+                    rhs=adj_of[g * ROW_GROUPS + u][:, :, c * FOLD : (c + 1) * FOLD],
+                    start=(c == 0),
+                    stop=(c == NODES // FOLD - 1),
+                )
 
         def sum_folded(g):
             nc.vector.tensor_reduce(
@@ -219,7 +218,7 @@ def tile_cheblayer_pa_t_kernel(tc, x, adj, out):
             s, n = divmod(q, PARTS_PER_PASS)
             if m not in x_grouped_of:
                 x_grouped_of[m] = x_stage.tile(
-                    [P, X_WIDTH, PACK], BF16, align_bytes=64, name="grouped"
+                    [P, X_WIDTH, PACK], BF16, align_bytes=256, name="grouped"
                 )
             copy = nc.scalar.copy if engine == "scalar" else nc.vector.tensor_copy
             copy(
@@ -235,8 +234,8 @@ def tile_cheblayer_pa_t_kernel(tc, x, adj, out):
             g, q = divmod(m, PARTS)
             s, n = divmod(q, PARTS_PER_PASS)
             if q == 0:
-                x_codes = x_mx.tile([P, PASSES, FEATURES], U32, align_bytes=64)
-                x_scales = x_mx.tile([P, PASSES, FEATURES], U8, align_bytes=64)
+                x_codes = x_mx.tile([P, PASSES, FEATURES], U32, align_bytes=256)
+                x_scales = x_mx.tile([P, PASSES, FEATURES], U8, align_bytes=256)
                 x_mx_of[g] = (x_codes, x_scales)
             x_codes, x_scales = x_mx_of[g]
             cols = slice(n * X_WIDTH, (n + 1) * X_WIDTH)
@@ -282,7 +281,7 @@ def tile_cheblayer_pa_t_kernel(tc, x, adj, out):
             )
             if k == 0:
                 turned_of[n] = lap_stage.tile(
-                    [P, GROUP, PASSES, P, HALVES], F32, align_bytes=64, name="turned_rows"
+                    [P, GROUP, PASSES, P, HALVES], F32, align_bytes=256, name="turned_rows"
                 )
             turned = turn_psum.tile([P, PASSES, HALVES, P], F32, tag="turn")
             for s in range(PASSES):
@@ -295,8 +294,8 @@ def tile_cheblayer_pa_t_kernel(tc, x, adj, out):
 
         def quantise_blocks(n, first, last):
             width = (last + 1 - first) * PASSES * P
-            codes = lap_mx.tile([P, width], U32, align_bytes=64, tag=f"codes{width}")
-            scales = lap_mx.tile([P, width], U8, align_bytes=64, tag=f"scales{width}")
+            codes = lap_mx.tile([P, width], U32, align_bytes=256, tag=f"codes{width}")
+            scales = lap_mx.tile([P, width], U8, align_bytes=256, tag=f"scales{width}")
             nc.vector.quantize_mx(
                 out=codes[:].bitcast(FP8X4),
                 scales=scales[:],
@@ -332,12 +331,15 @@ def tile_cheblayer_pa_t_kernel(tc, x, adj, out):
                 result_of[n, k] = out_pool.tile([P, FEATURES], F32, name="result")
                 left_of[n, k] = FEATURE_TILES
             result = result_of[n, k]
-            copy(out=result[:, f * BANK : (f + 1) * BANK], in_=acc_of[n, k][f][:])
+            cols = slice(f * BANK, (f + 1) * BANK)
+            copy(out=result[:, cols], in_=acc_of[n, k][f][:])
+            g, u = divmod(n, ROW_GROUPS)
+            rows = slice((u * GROUP + k) * P, (u * GROUP + k + 1) * P)
             left_of[n, k] -= 1
-            if left_of[n, k] == 0:
-                g, u = divmod(n, ROW_GROUPS)
-                first_row = (u * GROUP + k) * P
-                nc.sync.dma_start(out=out[g, first_row : first_row + P, :], in_=result[:])
+            if n == STEPS - 1 and k == GROUP - 1:
+                nc.sync.dma_start(out=out[g, rows, cols], in_=result[:, cols])
+            elif left_of[n, k] == 0:
+                nc.sync.dma_start(out=out[g, rows, :], in_=result[:])
 
         folded_of, x_mx_of, scales_of = {}, {}, {}
         x_grouped_of = {}

from contextlib import ExitStack

import concourse.mybir as mybir
from concourse.masks import make_identity

F32 = mybir.dt.float32
BF16 = mybir.dt.bfloat16
U32 = mybir.dt.uint32
U8 = mybir.dt.uint8
FP8X4 = mybir.dt.float8_e4m3fn_x4
ALU = mybir.AluOpType
ACT = mybir.ActivationFunctionType

GRAPHS = 4
NODES = 1024
FEATURES = 1024
EPS = 1e-6

P = 128
PACK = 4
K_PASS = P * PACK
PASSES = NODES // K_PASS
PAIR = 2
HALVES = PACK // PAIR
ROW_BLOCKS = NODES // P
GROUP = 2
ROW_GROUPS = ROW_BLOCKS // GROUP
STEPS = GRAPHS * ROW_GROUPS
BANK = 512
FEATURE_TILES = FEATURES // BANK

X_TILES = 2 * PASSES
FOLD = 64
PARTS = 4
PARTS_PER_PASS = PARTS // PASSES
X_WIDTH = FEATURES // PARTS_PER_PASS
DIAGONAL_STEP = NODES + P
S_COLUMNS = 208
HEAD_COLUMNS = {0: 0, 1: X_WIDTH, 2: X_WIDTH, 3: X_WIDTH}
X_LEAD = PARTS - 1
FOLD_LEAD = ROW_GROUPS + 3
ADJ_TILES = 12
LANE = 8
IN_FLIGHT = 6

FLOPS = 2 * GRAPHS * NODES * NODES * FEATURES


def scalar_columns(m):
    return HEAD_COLUMNS.get(m, S_COLUMNS)


def sum_column(g, b):
    return b if g > 0 else b // 2 + LANE * (b % 2)


def tile_cheblayer_pa_t_kernel(tc, x, adj, out):
    nc = tc.nc
    with ExitStack() as ctx:
        const = ctx.enter_context(tc.tile_pool(name="const", bufs=1))
        adj_pool = ctx.enter_context(tc.tile_pool(name="adj", bufs=ADJ_TILES))
        x_pool = ctx.enter_context(tc.tile_pool(name="x", bufs=X_TILES))
        sum_pool = ctx.enter_context(tc.tile_pool(name="sums", bufs=GRAPHS))
        small = ctx.enter_context(tc.tile_pool(name="small", bufs=2))
        unread = ctx.enter_context(tc.tile_pool(name="unread", bufs=2))
        row_pool = ctx.enter_context(tc.tile_pool(name="r_row", bufs=2))
        diag_pool = ctx.enter_context(tc.tile_pool(name="diag", bufs=2))
        x_stage = ctx.enter_context(tc.tile_pool(name="x_stage", bufs=5))
        x_mx = ctx.enter_context(tc.tile_pool(name="x_mx", bufs=2))
        lap_stage = ctx.enter_context(tc.tile_pool(name="lap_stage", bufs=IN_FLIGHT // GROUP))
        lap_mx = ctx.enter_context(tc.tile_pool(name="lap_mx", bufs=IN_FLIGHT // GROUP))
        out_pool = ctx.enter_context(tc.tile_pool(name="out", bufs=10))
        turn_psum = ctx.enter_context(tc.psum_pool(name="turn", bufs=3))
        fold_psum = ctx.enter_context(tc.psum_pool(name="fold", bufs=1))
        acc_psum = ctx.enter_context(tc.psum_pool(name="acc", bufs=4))

        ctx.enter_context(tc.manual_schedule())

        ident = const.tile([P, P], F32)
        make_identity(nc, ident[:])
        ident_bf16 = const.tile([P, P], BF16)
        nc.vector.tensor_copy(out=ident_bf16[:], in_=ident[:])
        eps = const.tile([P, 1], F32)
        nc.vector.memset(eps[:], EPS)

        warm = const.tile([P, 1], F32)
        nc.scalar.activation(out=warm[:], in_=eps[:], func=ACT.Abs_reciprocal_sqrt)

        adj_of, diagonal_of = {}, {}
        x_of, sums_of = {}, []
        for g in range(GRAPHS):
            sums = sum_pool.tile([P, 2 * LANE], F32)
            nc.vector.memset(sums[:], 1.0)
            sums_of.append(sums)

        def load_rows(n):
            if n < STEPS:
                g, u = divmod(n, ROW_GROUPS)
                flat = adj_pool.tile([P, GROUP * DIAGONAL_STEP], BF16)
                rows = flat[:, : GROUP * NODES].rearrange("p (k j) -> p k j", k=GROUP)
                nc.sync.dma_start(
                    out=rows,
                    in_=adj[g, u * GROUP * P : (u + 1) * GROUP * P, :].rearrange(
                        "(b p) j -> p b j", p=P
                    ),
                )
                adj_of[n] = rows
                first = u * GROUP * P
                diagonal_of[n] = flat[:].rearrange("p (k y) -> p k y", k=GROUP)[
                    :, :, first : first + P
                ]

        def load_x(n):
            if n < GRAPHS * PASSES:
                g, s = divmod(n, PASSES)
                x_sb = x_pool.tile([P, PACK, FEATURES], BF16)
                nc.sync.dma_start(
                    out=x_sb[:],
                    in_=x[g, s * K_PASS : (s + 1) * K_PASS, :].rearrange("(p t) f -> p t f", t=PACK),
                )
                x_of[n] = x_sb

        def sum_rows(u):
            for k in range(GROUP):
                column = sum_column(0, u * GROUP + k)
                total = sums_of[0][:, column : column + 1]
                if k == 0:
                    scalar_copy = unread.tile([P, NODES], BF16)
                    nc.scalar.activation(
                        out=scalar_copy[:], in_=adj_of[u][:, k, :], func=ACT.Copy, accum_out=total
                    )
                else:
                    vector_copy = unread.tile([P, NODES], BF16)
                    nc.vector.tensor_scalar(
                        out=vector_copy[:], in0=adj_of[u][:, k, :], scalar1=1.0, scalar2=None,
                        op0=ALU.mult, op1=ALU.add, accum_out=total,
                    )

        def fold_rows(g, u):
            if u == 0:
                folded_of[g] = fold_psum.tile([P, ROW_BLOCKS, FOLD], F32, name="folded")
            for c in range(NODES // FOLD):
                nc.tensor.matmul(
                    out=folded_of[g][:, u * GROUP : (u + 1) * GROUP, :],
                    lhsT=ident_bf16[:],
                    rhs=adj_of[g * ROW_GROUPS + u][:, :, c * FOLD : (c + 1) * FOLD],
                    start=(c == 0),
                    stop=(c == NODES // FOLD - 1),
                )

        def sum_folded(g):
            nc.vector.tensor_reduce(
                out=sums_of[g][:, :ROW_BLOCKS], in_=folded_of[g][:],
                axis=mybir.AxisListType.X, op=ALU.add,
            )

        def guess_scales(g):
            guess = small.tile([P, 2 * LANE], F32)
            nc.scalar.activation(
                out=guess[:], in_=sums_of[g][:], func=ACT.Abs_reciprocal_sqrt, bias=eps[:]
            )
            return guess

        def refine_scales(g, guess):
            half_sq = small.tile([P, 2 * LANE], F32)
            nc.vector.scalar_tensor_tensor(
                out=half_sq[:], in0=guess[:], scalar=0.5, in1=guess[:], op0=ALU.mult, op1=ALU.mult
            )
            near_half = small.tile([P, 2 * LANE], F32)
            nc.vector.scalar_tensor_tensor(
                out=near_half[:], in0=sums_of[g][:], scalar=EPS, in1=half_sq[:],
                op0=ALU.add, op1=ALU.mult,
            )
            neg_r = small.tile([P, 2 * LANE], F32)
            nc.vector.scalar_tensor_tensor(
                out=neg_r[:], in0=near_half[:], scalar=1.5, in1=guess[:],
                op0=ALU.subtract, op1=ALU.mult,
            )
            return neg_r

        def spread_scales(g, neg_r):
            blocks_per_bank = BANK // P
            spreads = []
            for h in range(NODES // BANK):
                spread = turn_psum.tile([P, blocks_per_bank, P], F32, tag="turn")
                for q in range(blocks_per_bank):
                    column = sum_column(g, h * blocks_per_bank + q)
                    nc.tensor.transpose(
                        spread[:, q, :],
                        neg_r[:, column : column + 1].to_broadcast([P, P]),
                        ident[:],
                    )
                spreads.append(spread)
            return spreads

        def copy_scales(g, spreads):
            r_row = row_pool.tile([P, NODES], F32)
            for h, spread in enumerate(spreads):
                to = r_row[:, h * BANK : (h + 1) * BANK]
                source = spread[:].rearrange("p q n -> p (q n)")
                if g == 0:
                    nc.vector.tensor_scalar_mul(out=to, in0=source, scalar1=-1.0)
                else:
                    nc.scalar.mul(out=to, in_=source, mul=-1.0)
            return r_row

        def lay_out(m, engine, half=None):
            if m >= GRAPHS * PARTS:
                return
            mid = X_WIDTH - scalar_columns(m)
            lo, hi = (mid, X_WIDTH) if engine == "scalar" else (0, mid)
            if half is not None:
                cut = lo + (hi - lo) // 2 // 16 * 16
                lo, hi = ((lo, cut), (cut, hi))[half]
            if lo == hi:
                return
            g, q = divmod(m, PARTS)
            s, n = divmod(q, PARTS_PER_PASS)
            if m not in x_grouped_of:
                x_grouped_of[m] = x_stage.tile(
                    [P, X_WIDTH, PACK], BF16, align_bytes=256, name="grouped"
                )
            copy = nc.scalar.copy if engine == "scalar" else nc.vector.tensor_copy
            copy(
                out=x_grouped_of[m][:, lo:hi].rearrange("p (c i) t -> p c t i", i=4),
                in_=x_of[g * PASSES + s][:, :, n * X_WIDTH + lo : n * X_WIDTH + hi].rearrange(
                    "p t (c i) -> p c t i", i=4
                ),
            )

        def quantise_part(m):
            if m >= GRAPHS * PARTS:
                return
            g, q = divmod(m, PARTS)
            s, n = divmod(q, PARTS_PER_PASS)
            if q == 0:
                x_codes = x_mx.tile([P, PASSES, FEATURES], U32, align_bytes=256)
                x_scales = x_mx.tile([P, PASSES, FEATURES], U8, align_bytes=256)
                x_mx_of[g] = (x_codes, x_scales)
            x_codes, x_scales = x_mx_of[g]
            cols = slice(n * X_WIDTH, (n + 1) * X_WIDTH)
            nc.vector.quantize_mx(
                out=x_codes[:, s, cols].bitcast(FP8X4),
                scales=x_scales[:, s, cols],
                in_=x_grouped_of[m][:].rearrange("p f t -> p (f t)"),
            )

        def form_products(n):
            g, u = divmod(n, ROW_GROUPS)
            products_of[n] = diag_pool.tile([P, GROUP, P], F32, name="products")
            nc.vector.tensor_tensor(
                out=products_of[n][:],
                in0=diagonal_of[n],
                in1=scales_of[g][1][:, u * GROUP * P : (u + 1) * GROUP * P].rearrange(
                    "p (k j) -> p k j", k=GROUP
                ),
                op=ALU.mult,
            )

        def form_block(n, k):
            g, u = divmod(n, ROW_GROUPS)
            neg_r, r_row = scales_of[g]
            b = u * GROUP + k
            row = adj_of[n][:, k, :]
            for lo, hi in ((0, b * P), ((b + 1) * P, NODES)):
                if lo < hi:
                    nc.vector.scalar_tensor_tensor(
                        out=row[:, lo:hi], in0=row[:, lo:hi],
                        scalar=neg_r[:, sum_column(g, b) : sum_column(g, b) + 1],
                        in1=r_row[:, lo:hi], op0=ALU.mult, op1=ALU.mult,
                    )
            nc.vector.scalar_tensor_tensor(
                out=row[:, b * P : (b + 1) * P], in0=products_of[n][:, k, :],
                scalar=neg_r[:, sum_column(g, b) : sum_column(g, b) + 1],
                in1=ident[:], op0=ALU.mult, op1=ALU.add,
            )

        def turn_block(n, k):
            words = adj_of[n][:].bitcast(F32).rearrange(
                "p b (s w h) -> p b s h w", s=PASSES, h=HALVES
            )
            if k == 0:
                turned_of[n] = lap_stage.tile(
                    [P, GROUP, PASSES, P, HALVES], F32, align_bytes=256, name="turned_rows"
                )
            turned = turn_psum.tile([P, PASSES, HALVES, P], F32, tag="turn")
            for s in range(PASSES):
                for h in range(HALVES):
                    nc.tensor.transpose(turned[:, s, h, :], words[:, k, s, h, :], ident[:])
            bank_of[n, k] = turned

        def move_turned(n, k, copy):
            copy(out=turned_of[n][:, k], in_=bank_of[n, k][:].rearrange("p s h m -> p s m h"))

        def quantise_blocks(n, first, last):
            width = (last + 1 - first) * PASSES * P
            codes = lap_mx.tile([P, width], U32, align_bytes=256, tag=f"codes{width}")
            scales = lap_mx.tile([P, width], U8, align_bytes=256, tag=f"scales{width}")
            nc.vector.quantize_mx(
                out=codes[:].bitcast(FP8X4),
                scales=scales[:],
                in_=turned_of[n][:, first : last + 1]
                .rearrange("p b s m h -> p (b s m h)")
                .bitcast(BF16),
            )
            for k in range(first, last + 1):
                mine = slice((k - first) * PASSES * P, (k + 1 - first) * PASSES * P)
                lap_of[n, k] = (codes[:, mine], scales[:, mine])

        def multiply_block(n, k):
            codes, scales = lap_of[n, k]
            x_codes, x_scales = x_mx_of[n // ROW_GROUPS]
            acc_of[n, k] = []
            for f in range(FEATURE_TILES):
                cols = slice(f * BANK, (f + 1) * BANK)
                acc = acc_psum.tile([P, BANK], F32)
                for s in range(PASSES):
                    nc.tensor.matmul_mx(
                        out=acc[:],
                        lhsT=codes[:, s * P : (s + 1) * P].bitcast(FP8X4),
                        lhsT_scale=scales[:, s * P : (s + 1) * P],
                        rhs=x_codes[:, s, cols].bitcast(FP8X4),
                        rhs_scale=x_scales[:, s, cols],
                        start=(s == 0),
                        stop=(s == PASSES - 1),
                    )
                acc_of[n, k].append(acc)

        def copy_result(n, k, f, copy):
            if (n, k) not in result_of:
                result_of[n, k] = out_pool.tile([P, FEATURES], F32, name="result")
                left_of[n, k] = FEATURE_TILES
            result = result_of[n, k]
            cols = slice(f * BANK, (f + 1) * BANK)
            copy(out=result[:, cols], in_=acc_of[n, k][f][:])
            g, u = divmod(n, ROW_GROUPS)
            rows = slice((u * GROUP + k) * P, (u * GROUP + k + 1) * P)
            left_of[n, k] -= 1
            if n == STEPS - 1 and k == GROUP - 1:
                nc.sync.dma_start(out=out[g, rows, cols], in_=result[:, cols])
            elif left_of[n, k] == 0:
                nc.sync.dma_start(out=out[g, rows, :], in_=result[:])

        folded_of, x_mx_of, scales_of = {}, {}, {}
        x_grouped_of = {}
        products_of, turned_of = {}, {}
        bank_of, lap_of, acc_of, result_of, left_of = {}, {}, {}, {}, {}
        on_scalar, on_vector = nc.scalar.copy, nc.vector.tensor_copy

        for n in range(ROW_GROUPS):
            load_rows(n)
        for n in range(PASSES):
            load_x(n)
        load_rows(ROW_GROUPS)
        load_rows(ROW_GROUPS + 1)
        load_x(PASSES)
        for n in range(ROW_GROUPS + 2, 2 * ROW_GROUPS):
            load_rows(n)
        load_x(PASSES + 1)
        for n in range(2 * ROW_GROUPS, ADJ_TILES):
            load_rows(n)

        for u in range(ROW_GROUPS):
            sum_rows(u)
        guess = guess_scales(0)
        neg_r = refine_scales(0, guess)
        spreads = spread_scales(0, neg_r)
        lay_out(0, "vector")
        for m in range(PARTS):
            lay_out(m, "scalar")
        scales_of[0] = (neg_r, copy_scales(0, spreads))
        fold_rows(1, 0)

        load_x(X_TILES)

        for step in range(STEPS):
            fold_g, fold_u = divmod(step + FOLD_LEAD, ROW_GROUPS)
            due_g, due = divmod(step + 3, ROW_GROUPS)
            due_g = due_g if 1 <= due_g < GRAPHS else 0
            final = step == STEPS - 1

            form_products(step)
            form_block(step, 0)
            turn_block(step, 0)
            move_turned(step, 0, on_scalar)
            if due_g and due == 1:
                guess = guess_scales(due_g)
            if due_g and due == 2:
                spreads = spread_scales(due_g, neg_r)
            if due_g and due == 2:
                scales_of[due_g] = (neg_r, copy_scales(due_g, spreads))
            lay_out(step + X_LEAD + 1, "scalar")
            form_block(step, 1)
            turn_block(step, 1)
            move_turned(step, 1, on_scalar)
            if step > 0:
                quantise_blocks(step - 1, 0, GROUP - 1)
            if step > 0:
                multiply_block(step - 1, 0)
            if step > 0:
                copy_result(step - 1, 0, 0, on_scalar)
            if step > 0 and not final:
                copy_result(step - 1, 0, 1, on_scalar)
            if step > 0:
                multiply_block(step - 1, 1)
            if step > 0:
                copy_result(step - 1, 1, 0, on_scalar)
            if step > 0 and not final:
                copy_result(step - 1, 1, 1, on_scalar)
            if step == 0:
                quantise_part(0)
                lay_out(3, "vector")
                quantise_part(1)
                quantise_part(2)
            quantise_part(step + X_LEAD)
            if due_g and due == 0:
                sum_folded(due_g)
            lay_out(step + X_LEAD + 1, "vector")
            if due_g and due == 1:
                neg_r = refine_scales(due_g, guess)
            if step == 0:
                for u in range(1, ROW_GROUPS):
                    fold_rows(1, u)
            elif fold_g < GRAPHS:
                fold_rows(fold_g, fold_u)
            load_rows(step + ADJ_TILES)
            if (step + X_LEAD) % 2 == 1:
                load_x((step + X_LEAD) // 2 + X_TILES)

        n = STEPS - 1
        quantise_blocks(n, 0, 0)
        copy_result(n - 1, 0, 1, on_vector)
        quantise_blocks(n, 1, 1)
        copy_result(n - 1, 1, 1, on_vector)
        for k in range(GROUP):
            multiply_block(n, k)
            copy_result(n, k, 0, on_scalar)
            copy_result(n, k, 1, on_vector)
